import numpy as np
import ml_dtypes


def mxq(x, axis, fmt="e4m3"):
    dtype, down = {"e4m3": (ml_dtypes.float8_e4m3fn, 7), "e5m2": (ml_dtypes.float8_e5m2, 14)}[fmt]
    v = np.moveaxis(np.asarray(x, np.float32).astype(ml_dtypes.bfloat16).astype(np.float64), axis, -1)
    blocks = v.reshape(v.shape[:-1] + (-1, 32))
    amax = np.abs(blocks).max(-1, keepdims=True)
    byte = np.maximum(np.where(amax > 0, np.frexp(amax)[1] - 1 + 127, 0) - down, 1)
    scale = np.exp2(byte - 127.0)
    codes = (blocks / scale).astype(np.float32).astype(dtype).astype(np.float64)
    return np.moveaxis((codes * scale).reshape(v.shape), -1, axis)


WIDE = False


def mx_kscale(k):
    if not WIDE:
        return np.ones(k)
    levels = np.array([10, -10, 5, -5, 0])
    a = np.random.permutation(np.resize(levels, k // 512 * 4)).reshape(k // 512, 4)
    idx = np.arange(k)
    return np.exp2(a[idx // 512, idx % 128 // 32])


BF16 = ml_dtypes.bfloat16


def bf(x):
    return np.asarray(x, np.float32).astype(BF16)


def f64(x):
    return np.asarray(x).astype(np.float64)


N, P, D, E, F = 5120, 3, 512, 512, 128
BN_EPS = 1e-5


def setup_inputs():
    t = mx_kscale(E)
    h = 1.2 * np.random.standard_normal((N, P, E)) + 0.6 * np.random.standard_normal((1, P, E))
    return {"h_sage": bf(h * t),
            "w1b": bf(np.random.standard_normal((E, F)) / np.sqrt(E) / t[:, None]),
            "w2b": bf(np.random.standard_normal((E, F)) / np.sqrt(E) / t[:, None]),
            "gamma": bf(1.0 + 0.2 * np.random.standard_normal(F)),
            "beta": bf(0.3 * np.random.standard_normal(F))}


def reference(h_sage, w1b, w2b, gamma, beta):
    h = f64(h_sage)
    neigh = (h.sum(axis=1, keepdims=True) - h) * 0.5
    out = (mxq(h[:, 0, :], 1, "e4m3") @ mxq(f64(w2b), 0, "e4m3")) + (mxq(neigh[:, 0, :], 1, "e4m3") @ mxq(f64(w1b), 0, "e4m3"))
    mean = out.mean(axis=0)
    var = out.var(axis=0)
    out = (out - mean) / np.sqrt(var + BN_EPS) * f64(gamma) + f64(beta)
    return 1.0 / (1.0 + np.exp(-out))

@@ -1,0 +1,220 @@
+from contextlib import ExitStack
+
+import concourse.mybir as mybir
+from concourse.masks import make_identity
+
+BF16 = mybir.dt.bfloat16
+F32 = mybir.dt.float32
+U32 = mybir.dt.uint32
+U8 = mybir.dt.uint8
+FP8X4 = mybir.dt.float8_e4m3fn_x4
+ALU = mybir.AluOpType
+ACT = mybir.ActivationFunctionType
+
+P = 128
+PACK = 4
+HALVES = 2
+PAIR = 2
+ITEMS = 5120
+HOPS = 3
+FEATS = 512
+COLS = 128
+BN_EPS = 1e-5
+BN_STATS_DIM = 6
+
+TILES = ITEMS // P
+BANK_TILES = 2
+PIECES = (1, 1, 2) + (4,) * 8 + (2, 1, 1)
+Y_KEPT = 4
+assert sum(PIECES) == TILES
+
+FLOPS = 2 * 2 * ITEMS * FEATS * COLS
+
+
+def tile_dogtaitujuanji_pb_t_kernel(tc, h_sage, w1b, w2b, gamma, beta, out):
+    nc = tc.nc
+    h_rows = h_sage.rearrange("(p j) q k -> p j q k", j=TILES)
+    out_rows = out.rearrange("(p j) f -> p j f", j=TILES)
+    first_tile = [sum(PIECES[:i]) for i in range(len(PIECES))]
+
+    with ExitStack() as ctx:
+        ctx.enter_context(tc.manual_schedule())
+        const = ctx.enter_context(tc.tile_pool(name="const", bufs=1))
+        h_pool = ctx.enter_context(tc.tile_pool(name="h", bufs=1))
+        y_pool = ctx.enter_context(tc.tile_pool(name="y_sbuf", bufs=1))
+        grouped = ctx.enter_context(tc.tile_pool(name="grouped", bufs=3))
+        packed = ctx.enter_context(tc.tile_pool(name="packed", bufs=3))
+        result = ctx.enter_context(tc.tile_pool(name="result", bufs=3))
+        psum_turn = ctx.enter_context(tc.psum_pool(name="psum_turn", bufs=4))
+        psum_y = ctx.enter_context(tc.psum_pool(name="psum_y", bufs=Y_KEPT))
+
+        h_pieces = []
+        for i, n_tiles in enumerate(PIECES):
+            h_piece = h_pool.tile([P, n_tiles, HOPS, FEATS], BF16, name="h_piece%d" % i)
+            nc.sync.dma_start(
+                out=h_piece[:], in_=h_rows[:, first_tile[i] : first_tile[i] + n_tiles]
+            )
+            h_pieces.append(h_piece)
+
+        w_raw = const.tile([P, 2, PACK, COLS], BF16)
+        for i, w in enumerate((w2b, w1b)):
+            nc.scalar.dma_start(
+                out=w_raw[:, i].rearrange("p (u e) f -> p u (e f)", u=HALVES),
+                in_=w.rearrange("(u p e) f -> p u (e f)", u=HALVES, e=PAIR),
+            )
+        gamma_bf = const.tile([P, 1], BF16)
+        beta_bf = const.tile([P, 1], BF16)
+        nc.scalar.dma_start(out=gamma_bf[:], in_=gamma.rearrange("(f o) -> f o", o=1))
+        nc.scalar.dma_start(out=beta_bf[:], in_=beta.rearrange("(f o) -> f o", o=1))
+
+        ident = const.tile([P, P], F32)
+        make_identity(nc, ident[:])
+        minus_half = const.tile([P, 1], F32)
+        nc.vector.memset(minus_half[:], -0.5)
+        warm = const.tile([P, 1], F32)
+        nc.vector.memset(warm[:], 0.0)
+        nc.scalar.activation(out=warm[:], in_=warm[:], func=ACT.Sigmoid)
+
+        w_grouped = const.tile([P, 2, COLS, PACK], BF16, align_bytes=64)
+        nc.vector.tensor_copy(out=w_grouped[:], in_=w_raw[:].rearrange("p i t f -> p i f t"))
+        w_codes = const.tile([P, 2 * COLS], U32, align_bytes=64)
+        w_scales = const.tile([P, 2 * COLS], U8, align_bytes=64)
+        nc.vector.quantize_mx(
+            out=w_codes[:].bitcast(FP8X4),
+            scales=w_scales[:],
+            in_=w_grouped[:].rearrange("p i f t -> p (i f t)"),
+        )
+        stats = const.tile([P, len(PIECES), BN_STATS_DIM], F32)
+
+        def transpose_hop(h_piece, hop, first, count):
+            bank = psum_turn.tile([P, HALVES * count * P], F32, tag="turn")
+            for g in range(count):
+                words = h_piece[:, first + g, hop, :].bitcast(F32)
+                for u in range(HALVES):
+                    at = (u * count + g) * P
+                    nc.tensor.transpose(
+                        bank[:, at : at + P], words[:, u * P : (u + 1) * P], ident[:]
+                    )
+            return bank
+
+        def as_words(tile_bf16):
+            return tile_bf16[:].bitcast(F32).rearrange("p (c u) -> p c u", u=HALVES)
+
+        def as_pairs(tile_bf16):
+            return tile_bf16[:].rearrange("p (c u e) -> p c u e", u=HALVES, e=PAIR)
+
+        def quantise_piece(i):
+            h_piece = h_pieces[i]
+            n_tiles = PIECES[i]
+            width = n_tiles * P
+            self_t = grouped.tile([P, width * PACK], BF16, tag="self_t", align_bytes=64)
+            hop2_t = grouped.tile([P, width * PACK], BF16, tag="hop2_t", align_bytes=64)
+            neigh_t = grouped.tile([P, width * PACK], BF16, tag="neigh_t", align_bytes=64)
+            bank_starts = range(0, n_tiles, BANK_TILES)
+
+            for first in bank_starts:
+                count = min(BANK_TILES, n_tiles - first)
+                cols = slice(first * P, (first + count) * P)
+                bank2 = transpose_hop(h_piece, 2, first, count)
+                nc.scalar.copy(
+                    out=as_words(hop2_t)[:, cols, :],
+                    in_=bank2[:].rearrange("p (u c) -> p c u", u=HALVES),
+                )
+                bank1 = transpose_hop(h_piece, 1, first, count)
+                nc.vector.tensor_tensor(
+                    out=as_pairs(neigh_t)[:, cols],
+                    in0=bank1[:]
+                    .bitcast(BF16)
+                    .rearrange("p (u c e) -> p c u e", u=HALVES, e=PAIR),
+                    in1=as_pairs(hop2_t)[:, cols],
+                    op=ALU.add,
+                )
+            for first in bank_starts:
+                count = min(BANK_TILES, n_tiles - first)
+                cols = slice(first * P, (first + count) * P)
+                bank0 = transpose_hop(h_piece, 0, first, count)
+                nc.scalar.copy(
+                    out=as_words(self_t)[:, cols, :],
+                    in_=bank0[:].rearrange("p (u c) -> p c u", u=HALVES),
+                )
+            nc.vector.tensor_scalar_mul(out=neigh_t[:], in0=neigh_t[:], scalar1=0.5)
+
+            codes = {}
+            for name, values in (("self", self_t), ("neigh", neigh_t)):
+                words = packed.tile([P, width], U32, tag=name + "_codes", align_bytes=64)
+                scales = packed.tile([P, width], U8, tag=name + "_scales", align_bytes=64)
+                nc.vector.quantize_mx(out=words[:].bitcast(FP8X4), scales=scales[:], in_=values[:])
+                codes[name] = (words, scales)
+            return codes
+
+        def multiply_piece(i, codes):
+            width = PIECES[i] * P
+            y_psum = psum_y.tile([P, width], F32, tag="y")
+            for w_index, name in enumerate(("self", "neigh")):
+                words, scales = codes[name]
+                w_cols = slice(w_index * COLS, (w_index + 1) * COLS)
+                nc.tensor.matmul_mx(
+                    out=y_psum[:],
+                    lhsT=w_codes[:, w_cols].bitcast(FP8X4),
+                    lhsT_scale=w_scales[:, w_cols],
+                    rhs=words[:].bitcast(FP8X4),
+                    rhs_scale=scales[:],
+                    start=(w_index == 0),
+                    stop=(w_index == 1),
+                )
+            if i < len(PIECES) - Y_KEPT:
+                y_piece = y_pool.tile([P, width], F32, name="y_piece%d" % i)
+                nc.scalar.copy(out=y_piece[:], in_=y_psum[:])
+            else:
+                y_piece = y_psum
+            nc.vector.bn_stats(out=stats[:, i, :], in_=y_piece[:])
+            return y_piece
+
+        y_pieces = []
+        codes_before = quantise_piece(0)
+        gamma_f = const.tile([P, 1], F32)
+        neg_gamma_f = const.tile([P, 1], F32)
+        beta_f = const.tile([P, 1], F32)
+        nc.vector.tensor_copy(out=gamma_f[:], in_=gamma_bf[:])
+        nc.vector.tensor_scalar_mul(out=neg_gamma_f[:], in0=gamma_bf[:], scalar1=-1.0)
+        nc.vector.tensor_copy(out=beta_f[:], in_=beta_bf[:])
+        for i in range(1, len(PIECES)):
+            codes_now = quantise_piece(i)
+            y_pieces.append(multiply_piece(i - 1, codes_before))
+            codes_before = codes_now
+        y_pieces.append(multiply_piece(len(PIECES) - 1, codes_before))
+
+        mean_var = const.tile([P, 2], F32)
+        nc.vector.bn_aggr(out=mean_var[:], in_=stats[:].rearrange("p i s -> p (i s)"))
+        var_eps = const.tile([P, 1], F32)
+        nc.vector.tensor_scalar_add(out=var_eps[:], in0=mean_var[:, 1:2], scalar1=BN_EPS)
+        neg_gamma_mean = const.tile([P, 1], F32)
+        nc.vector.tensor_mul(out=neg_gamma_mean[:], in0=mean_var[:, 0:1], in1=neg_gamma_f[:])
+        rstd = const.tile([P, 1], F32)
+        nc.gpsimd.tensor_tensor(out=rstd[:], in0=var_eps[:], in1=minus_half[:], op=ALU.pow)
+        gain = const.tile([P, 1], F32)
+        nc.vector.tensor_mul(out=gain[:], in0=gamma_f[:], in1=rstd[:])
+        shift = const.tile([P, 1], F32)
+        nc.vector.tensor_scalar(
+            out=shift[:],
+            in0=neg_gamma_mean[:],
+            scalar1=rstd[:, 0:1],
+            scalar2=beta_f[:, 0:1],
+            op0=ALU.mult,
+            op1=ALU.add,
+        )
+
+        for i, n_tiles in enumerate(PIECES):
+            width = n_tiles * P
+            sig = result.tile([P, width], F32, tag="sig")
+            nc.scalar.activation(
+                out=sig[:], in_=y_pieces[i][:], func=ACT.Sigmoid, bias=shift[:, 0:1], scale=gain[:, 0:1]
+            )
+            back = psum_turn.tile([P, n_tiles, COLS], F32, tag="turn")
+            for g in range(n_tiles):
+                nc.tensor.transpose(back[:, g, :], sig[:, g * P : (g + 1) * P], ident[:])
+            rows = result.tile([P, n_tiles, COLS], F32, tag="rows")
+            nc.vector.tensor_copy(out=rows[:], in_=back[:])
+            nc.sync.dma_start(
+                out=out_rows[:, first_tile[i] : first_tile[i] + n_tiles, :], in_=rows[:]
+            )

@@ -25,7 +25,10 @@ BN_STATS_DIM = 6
 TILES = ITEMS // P
 BANK_TILES = 2
 PIECES = (1, 1, 2) + (4,) * 8 + (2, 1, 1)
-Y_KEPT = 4
+Y_KEPT = 3
+IDLE_WIDTH = 512
+WARM_PASSES = 6
+KEEP_PASSES = 2
 assert sum(PIECES) == TILES
 
 FLOPS = 2 * 2 * ITEMS * FEATS * COLS
@@ -47,6 +50,7 @@ def tile_dogtaitujuanji_pb_t_kernel(tc, h_sage, w1b, w2b, gamma, beta, out):
         result = ctx.enter_context(tc.tile_pool(name="result", bufs=3))
         psum_turn = ctx.enter_context(tc.psum_pool(name="psum_turn", bufs=4))
         psum_y = ctx.enter_context(tc.psum_pool(name="psum_y", bufs=Y_KEPT))
+        psum_idle = ctx.enter_context(tc.psum_pool(name="psum_idle", bufs=1))
 
         h_pieces = []
         for i, n_tiles in enumerate(PIECES):
@@ -74,6 +78,29 @@ def tile_dogtaitujuanji_pb_t_kernel(tc, h_sage, w1b, w2b, gamma, beta, out):
         warm = const.tile([P, 1], F32)
         nc.vector.memset(warm[:], 0.0)
         nc.scalar.activation(out=warm[:], in_=warm[:], func=ACT.Sigmoid)
+
+        idle_codes = const.tile([P, IDLE_WIDTH], U32, align_bytes=64)
+        idle_scales = const.tile([P, IDLE_WIDTH], U8, align_bytes=64)
+        idle_values = const.tile([P, IDLE_WIDTH * PACK], BF16, align_bytes=64)
+        nc.vector.memset(idle_values[:], 0.0)
+        nc.vector.quantize_mx(
+            out=idle_codes[:].bitcast(FP8X4), scales=idle_scales[:], in_=idle_values[:]
+        )
+        idle_out = psum_idle.tile([P, IDLE_WIDTH], F32)
+
+        def keep_clock(passes):
+            for n in range(passes):
+                nc.tensor.matmul_mx(
+                    out=idle_out[:],
+                    lhsT=idle_codes[:, :P].bitcast(FP8X4),
+                    lhsT_scale=idle_scales[:, :P],
+                    rhs=idle_codes[:].bitcast(FP8X4),
+                    rhs_scale=idle_scales[:],
+                    start=True,
+                    stop=True,
+                )
+
+        keep_clock(WARM_PASSES)
 
         w_grouped = const.tile([P, 2, COLS, PACK], BF16, align_bytes=64)
         nc.vector.tensor_copy(out=w_grouped[:], in_=w_raw[:].rearrange("p i t f -> p i f t"))
@@ -162,6 +189,7 @@ def tile_dogtaitujuanji_pb_t_kernel(tc, h_sage, w1b, w2b, gamma, beta, out):
                     start=(w_index == 0),
                     stop=(w_index == 1),
                 )
+            keep_clock(KEEP_PASSES)
             if i < len(PIECES) - Y_KEPT:
                 y_piece = y_pool.tile([P, width], F32, name="y_piece%d" % i)
                 nc.scalar.copy(out=y_piece[:], in_=y_psum[:])

@@ -25,10 +25,7 @@ BN_STATS_DIM = 6
 TILES = ITEMS // P
 BANK_TILES = 2
 PIECES = (1, 1, 2) + (4,) * 8 + (2, 1, 1)
-Y_KEPT = 3
-IDLE_WIDTH = 512
-WARM_PASSES = 6
-KEEP_PASSES = 2
+Y_KEPT = 4
 assert sum(PIECES) == TILES
 
 FLOPS = 2 * 2 * ITEMS * FEATS * COLS
@@ -38,7 +35,8 @@ def tile_dogtaitujuanji_pb_t_kernel(tc, h_sage, w1b, w2b, gamma, beta, out):
     nc = tc.nc
     h_rows = h_sage.rearrange("(p j) q k -> p j q k", j=TILES)
     out_rows = out.rearrange("(p j) f -> p j f", j=TILES)
-    first_tile = [sum(PIECES[:i]) for i in range(len(PIECES))]
+    n_pieces = len(PIECES)
+    first_tile = [sum(PIECES[:i]) for i in range(n_pieces)]
 
     with ExitStack() as ctx:
         ctx.enter_context(tc.manual_schedule())
@@ -50,7 +48,6 @@ def tile_dogtaitujuanji_pb_t_kernel(tc, h_sage, w1b, w2b, gamma, beta, out):
         result = ctx.enter_context(tc.tile_pool(name="result", bufs=3))
         psum_turn = ctx.enter_context(tc.psum_pool(name="psum_turn", bufs=4))
         psum_y = ctx.enter_context(tc.psum_pool(name="psum_y", bufs=Y_KEPT))
-        psum_idle = ctx.enter_context(tc.psum_pool(name="psum_idle", bufs=1))
 
         h_pieces = []
         for i, n_tiles in enumerate(PIECES):
@@ -61,46 +58,25 @@ def tile_dogtaitujuanji_pb_t_kernel(tc, h_sage, w1b, w2b, gamma, beta, out):
             h_pieces.append(h_piece)
 
         w_raw = const.tile([P, 2, PACK, COLS], BF16)
-        for i, w in enumerate((w2b, w1b)):
-            nc.scalar.dma_start(
-                out=w_raw[:, i].rearrange("p (u e) f -> p u (e f)", u=HALVES),
-                in_=w.rearrange("(u p e) f -> p u (e f)", u=HALVES, e=PAIR),
-            )
+        nc.scalar.dma_start(
+            out=w_raw[:, 0].rearrange("p (u e) f -> p u (e f)", u=HALVES),
+            in_=w2b.rearrange("(u p e) f -> p u (e f)", u=HALVES, e=PAIR),
+        )
+        nc.scalar.dma_start(out=w_raw[:, 1], in_=w1b.rearrange("(t p) f -> p t f", p=P))
         gamma_bf = const.tile([P, 1], BF16)
         beta_bf = const.tile([P, 1], BF16)
         nc.scalar.dma_start(out=gamma_bf[:], in_=gamma.rearrange("(f o) -> f o", o=1))
         nc.scalar.dma_start(out=beta_bf[:], in_=beta.rearrange("(f o) -> f o", o=1))
 
-        ident = const.tile([P, P], F32)
-        make_identity(nc, ident[:])
+        ident_f32 = const.tile([P, P], F32)
+        make_identity(nc, ident_f32[:])
+        ident_bf16 = const.tile([P, P], BF16)
+        make_identity(nc, ident_bf16[:])
         minus_half = const.tile([P, 1], F32)
         nc.vector.memset(minus_half[:], -0.5)
         warm = const.tile([P, 1], F32)
         nc.vector.memset(warm[:], 0.0)
         nc.scalar.activation(out=warm[:], in_=warm[:], func=ACT.Sigmoid)
-
-        idle_codes = const.tile([P, IDLE_WIDTH], U32, align_bytes=64)
-        idle_scales = const.tile([P, IDLE_WIDTH], U8, align_bytes=64)
-        idle_values = const.tile([P, IDLE_WIDTH * PACK], BF16, align_bytes=64)
-        nc.vector.memset(idle_values[:], 0.0)
-        nc.vector.quantize_mx(
-            out=idle_codes[:].bitcast(FP8X4), scales=idle_scales[:], in_=idle_values[:]
-        )
-        idle_out = psum_idle.tile([P, IDLE_WIDTH], F32)
-
-        def keep_clock(passes):
-            for n in range(passes):
-                nc.tensor.matmul_mx(
-                    out=idle_out[:],
-                    lhsT=idle_codes[:, :P].bitcast(FP8X4),
-                    lhsT_scale=idle_scales[:, :P],
-                    rhs=idle_codes[:].bitcast(FP8X4),
-                    rhs_scale=idle_scales[:],
-                    start=True,
-                    stop=True,
-                )
-
-        keep_clock(WARM_PASSES)
 
         w_grouped = const.tile([P, 2, COLS, PACK], BF16, align_bytes=64)
         nc.vector.tensor_copy(out=w_grouped[:], in_=w_raw[:].rearrange("p i t f -> p i f t"))
@@ -111,74 +87,72 @@ def tile_dogtaitujuanji_pb_t_kernel(tc, h_sage, w1b, w2b, gamma, beta, out):
             scales=w_scales[:],
             in_=w_grouped[:].rearrange("p i f t -> p (i f t)"),
         )
-        stats = const.tile([P, len(PIECES), BN_STATS_DIM], F32)
 
-        def transpose_hop(h_piece, hop, first, count):
-            bank = psum_turn.tile([P, HALVES * count * P], F32, tag="turn")
-            for g in range(count):
-                words = h_piece[:, first + g, hop, :].bitcast(F32)
-                for u in range(HALVES):
-                    at = (u * count + g) * P
-                    nc.tensor.transpose(
-                        bank[:, at : at + P], words[:, u * P : (u + 1) * P], ident[:]
-                    )
-            return bank
+        stats = const.tile([P, n_pieces, BN_STATS_DIM], F32)
 
-        def as_words(tile_bf16):
-            return tile_bf16[:].bitcast(F32).rearrange("p (c u) -> p c u", u=HALVES)
+        def banks_of(n_tiles):
+            return [(first, min(BANK_TILES, n_tiles - first)) for first in range(0, n_tiles, BANK_TILES)]
 
-        def as_pairs(tile_bf16):
-            return tile_bf16[:].rearrange("p (c u e) -> p c u e", u=HALVES, e=PAIR)
-
-        def quantise_piece(i):
+        def turn_piece(i):
             h_piece = h_pieces[i]
             n_tiles = PIECES[i]
-            width = n_tiles * P
-            self_t = grouped.tile([P, width * PACK], BF16, tag="self_t", align_bytes=64)
-            hop2_t = grouped.tile([P, width * PACK], BF16, tag="hop2_t", align_bytes=64)
-            neigh_t = grouped.tile([P, width * PACK], BF16, tag="neigh_t", align_bytes=64)
-            bank_starts = range(0, n_tiles, BANK_TILES)
+            sum_rows = grouped.tile([P, n_tiles, FEATS], BF16, tag="sum_rows")
+            nc.vector.tensor_tensor(
+                out=sum_rows[:], in0=h_piece[:, :, 1, :], in1=h_piece[:, :, 2, :], op=ALU.add
+            )
 
-            for first in bank_starts:
-                count = min(BANK_TILES, n_tiles - first)
-                cols = slice(first * P, (first + count) * P)
-                bank2 = transpose_hop(h_piece, 2, first, count)
+            self_t = grouped.tile([P, n_tiles * P * PACK], BF16, tag="self_t", align_bytes=64)
+            for first, count in banks_of(n_tiles):
+                bank = psum_turn.tile([P, HALVES * count * P], F32, tag="turn")
+                for g in range(count):
+                    words = h_piece[:, first + g, 0, :].bitcast(F32)
+                    for u in range(HALVES):
+                        at = (u * count + g) * P
+                        nc.tensor.transpose(
+                            bank[:, at : at + P], words[:, u * P : (u + 1) * P], ident_f32[:]
+                        )
                 nc.scalar.copy(
-                    out=as_words(hop2_t)[:, cols, :],
-                    in_=bank2[:].rearrange("p (u c) -> p c u", u=HALVES),
+                    out=self_t[:]
+                    .bitcast(F32)
+                    .rearrange("p (c u) -> p c u", u=HALVES)[:, first * P : (first + count) * P, :],
+                    in_=bank[:].rearrange("p (u c) -> p c u", u=HALVES),
                 )
-                bank1 = transpose_hop(h_piece, 1, first, count)
-                nc.vector.tensor_tensor(
-                    out=as_pairs(neigh_t)[:, cols],
-                    in0=bank1[:]
-                    .bitcast(BF16)
-                    .rearrange("p (u c e) -> p c u e", u=HALVES, e=PAIR),
-                    in1=as_pairs(hop2_t)[:, cols],
-                    op=ALU.add,
-                )
-            for first in bank_starts:
-                count = min(BANK_TILES, n_tiles - first)
-                cols = slice(first * P, (first + count) * P)
-                bank0 = transpose_hop(h_piece, 0, first, count)
-                nc.scalar.copy(
-                    out=as_words(self_t)[:, cols, :],
-                    in_=bank0[:].rearrange("p (u c) -> p c u", u=HALVES),
-                )
-            nc.vector.tensor_scalar_mul(out=neigh_t[:], in0=neigh_t[:], scalar1=0.5)
 
-            codes = {}
-            for name, values in (("self", self_t), ("neigh", neigh_t)):
+            neigh_t = grouped.tile([P, n_tiles * P * PACK], BF16, tag="neigh_t", align_bytes=64)
+            for first, count in banks_of(n_tiles):
+                bank = psum_turn.tile([P, count * PACK * P], BF16, tag="turn")
+                for g in range(count):
+                    for t in range(PACK):
+                        at = (g * PACK + t) * P
+                        nc.tensor.transpose(
+                            bank[:, at : at + P],
+                            sum_rows[:, first + g, t * P : (t + 1) * P],
+                            ident_bf16[:],
+                        )
+                nc.scalar.mul(
+                    out=neigh_t[:].rearrange("p (g c t) -> p g c t", c=P, t=PACK)[
+                        :, first : first + count
+                    ],
+                    in_=bank[:].rearrange("p (g t c) -> p g c t", g=count, t=PACK),
+                    mul=0.5,
+                )
+            return self_t, neigh_t
+
+        def quantise_piece(i, values):
+            width = PIECES[i] * P
+            operands = []
+            for name, tile_bf16 in zip(("self", "neigh"), values):
                 words = packed.tile([P, width], U32, tag=name + "_codes", align_bytes=64)
                 scales = packed.tile([P, width], U8, tag=name + "_scales", align_bytes=64)
-                nc.vector.quantize_mx(out=words[:].bitcast(FP8X4), scales=scales[:], in_=values[:])
-                codes[name] = (words, scales)
-            return codes
+                nc.vector.quantize_mx(
+                    out=words[:].bitcast(FP8X4), scales=scales[:], in_=tile_bf16[:]
+                )
+                operands.append((words, scales))
+            return operands
 
-        def multiply_piece(i, codes):
-            width = PIECES[i] * P
-            y_psum = psum_y.tile([P, width], F32, tag="y")
-            for w_index, name in enumerate(("self", "neigh")):
-                words, scales = codes[name]
+        def multiply_piece(i, operands):
+            y_psum = psum_y.tile([P, PIECES[i] * P], F32, tag="y")
+            for w_index, (words, scales) in enumerate(operands):
                 w_cols = slice(w_index * COLS, (w_index + 1) * COLS)
                 nc.tensor.matmul_mx(
                     out=y_psum[:],
@@ -189,40 +163,45 @@ def tile_dogtaitujuanji_pb_t_kernel(tc, h_sage, w1b, w2b, gamma, beta, out):
                     start=(w_index == 0),
                     stop=(w_index == 1),
                 )
-            keep_clock(KEEP_PASSES)
-            if i < len(PIECES) - Y_KEPT:
-                y_piece = y_pool.tile([P, width], F32, name="y_piece%d" % i)
-                nc.scalar.copy(out=y_piece[:], in_=y_psum[:])
-            else:
-                y_piece = y_psum
-            nc.vector.bn_stats(out=stats[:, i, :], in_=y_piece[:])
-            return y_piece
+            return y_psum
 
+        def measure_piece(i, y_psum):
+            nc.vector.bn_stats(out=stats[:, i, :], in_=y_psum[:])
+            if i >= n_pieces - Y_KEPT:
+                return y_psum
+            y_sbuf = y_pool.tile([P, PIECES[i] * P], F32, name="y_sbuf%d" % i)
+            nc.vector.tensor_copy(out=y_sbuf[:], in_=y_psum[:])
+            return y_sbuf
+
+        turned = {}
+        products = {}
         y_pieces = []
-        codes_before = quantise_piece(0)
+        for step in range(n_pieces + 2):
+            if step < n_pieces:
+                turned[step] = turn_piece(step)
+            if 1 <= step <= n_pieces:
+                operands = quantise_piece(step - 1, turned[step - 1])
+                products[step - 1] = multiply_piece(step - 1, operands)
+            if step >= 2:
+                y_pieces.append(measure_piece(step - 2, products[step - 2]))
+
         gamma_f = const.tile([P, 1], F32)
         neg_gamma_f = const.tile([P, 1], F32)
         beta_f = const.tile([P, 1], F32)
-        nc.vector.tensor_copy(out=gamma_f[:], in_=gamma_bf[:])
-        nc.vector.tensor_scalar_mul(out=neg_gamma_f[:], in0=gamma_bf[:], scalar1=-1.0)
-        nc.vector.tensor_copy(out=beta_f[:], in_=beta_bf[:])
-        for i in range(1, len(PIECES)):
-            codes_now = quantise_piece(i)
-            y_pieces.append(multiply_piece(i - 1, codes_before))
-            codes_before = codes_now
-        y_pieces.append(multiply_piece(len(PIECES) - 1, codes_before))
-
         mean_var = const.tile([P, 2], F32)
-        nc.vector.bn_aggr(out=mean_var[:], in_=stats[:].rearrange("p i s -> p (i s)"))
         var_eps = const.tile([P, 1], F32)
-        nc.vector.tensor_scalar_add(out=var_eps[:], in0=mean_var[:, 1:2], scalar1=BN_EPS)
         neg_gamma_mean = const.tile([P, 1], F32)
-        nc.vector.tensor_mul(out=neg_gamma_mean[:], in0=mean_var[:, 0:1], in1=neg_gamma_f[:])
         rstd = const.tile([P, 1], F32)
-        nc.gpsimd.tensor_tensor(out=rstd[:], in0=var_eps[:], in1=minus_half[:], op=ALU.pow)
         gain = const.tile([P, 1], F32)
-        nc.vector.tensor_mul(out=gain[:], in0=gamma_f[:], in1=rstd[:])
         shift = const.tile([P, 1], F32)
+        nc.vector.bn_aggr(out=mean_var[:], in_=stats[:].rearrange("p i s -> p (i s)"))
+        nc.vector.tensor_scalar_add(out=var_eps[:], in0=mean_var[:, 1:2], scalar1=BN_EPS)
+        nc.gpsimd.tensor_tensor(out=rstd[:], in0=var_eps[:], in1=minus_half[:], op=ALU.pow)
+        nc.vector.tensor_copy(out=gamma_f[:], in_=gamma_bf[:])
+        nc.vector.tensor_copy(out=beta_f[:], in_=beta_bf[:])
+        nc.vector.tensor_scalar_mul(out=neg_gamma_f[:], in0=gamma_bf[:], scalar1=-1.0)
+        nc.vector.tensor_mul(out=neg_gamma_mean[:], in0=mean_var[:, 0:1], in1=neg_gamma_f[:])
+        nc.vector.tensor_mul(out=gain[:], in0=gamma_f[:], in1=rstd[:])
         nc.vector.tensor_scalar(
             out=shift[:],
             in0=neg_gamma_mean[:],
@@ -233,14 +212,17 @@ def tile_dogtaitujuanji_pb_t_kernel(tc, h_sage, w1b, w2b, gamma, beta, out):
         )
 
         for i, n_tiles in enumerate(PIECES):
-            width = n_tiles * P
-            sig = result.tile([P, width], F32, tag="sig")
+            sig = result.tile([P, n_tiles * P], F32, tag="sig")
             nc.scalar.activation(
-                out=sig[:], in_=y_pieces[i][:], func=ACT.Sigmoid, bias=shift[:, 0:1], scale=gain[:, 0:1]
+                out=sig[:],
+                in_=y_pieces[i][:],
+                func=ACT.Sigmoid,
+                bias=shift[:, 0:1],
+                scale=gain[:, 0:1],
             )
             back = psum_turn.tile([P, n_tiles, COLS], F32, tag="turn")
             for g in range(n_tiles):
-                nc.tensor.transpose(back[:, g, :], sig[:, g * P : (g + 1) * P], ident[:])
+                nc.tensor.transpose(back[:, g, :], sig[:, g * P : (g + 1) * P], ident_f32[:])
             rows = result.tile([P, n_tiles, COLS], F32, tag="rows")
             nc.vector.tensor_copy(out=rows[:], in_=back[:])
             nc.sync.dma_start(

@@ -46,6 +46,7 @@ def tile_dogtaitujuanji_pb_t_kernel(tc, h_sage, w1b, w2b, gamma, beta, out):
         grouped = ctx.enter_context(tc.tile_pool(name="grouped", bufs=3))
         packed = ctx.enter_context(tc.tile_pool(name="packed", bufs=3))
         result = ctx.enter_context(tc.tile_pool(name="result", bufs=3))
+        rows_pool = ctx.enter_context(tc.tile_pool(name="rows", bufs=1))
         psum_turn = ctx.enter_context(tc.psum_pool(name="psum_turn", bufs=4))
         psum_y = ctx.enter_context(tc.psum_pool(name="psum_y", bufs=Y_KEPT))
 
@@ -223,7 +224,7 @@ def tile_dogtaitujuanji_pb_t_kernel(tc, h_sage, w1b, w2b, gamma, beta, out):
             back = psum_turn.tile([P, n_tiles, COLS], F32, tag="turn")
             for g in range(n_tiles):
                 nc.tensor.transpose(back[:, g, :], sig[:, g * P : (g + 1) * P], ident_f32[:])
-            rows = result.tile([P, n_tiles, COLS], F32, tag="rows")
+            rows = rows_pool.tile([P, n_tiles, COLS], F32, name="rows%d" % i)
             nc.vector.tensor_copy(out=rows[:], in_=back[:])
             nc.sync.dma_start(
                 out=out_rows[:, first_tile[i] : first_tile[i] + n_tiles, :], in_=rows[:]

@@ -24,7 +24,9 @@ BN_STATS_DIM = 6
 
 TILES = ITEMS // P
 BANK_TILES = 2
-PIECES = (1, 1, 2) + (4,) * 8 + (2, 1, 1)
+PIECES = (1, 1, 2) + (4,) * 9
+KEEP_PASSES = 2
+ZERO_WIDTH = 512
 Y_KEPT = 4
 assert sum(PIECES) == TILES
 
@@ -79,6 +81,14 @@ def tile_dogtaitujuanji_pb_t_kernel(tc, h_sage, w1b, w2b, gamma, beta, out):
         nc.vector.memset(warm[:], 0.0)
         nc.scalar.activation(out=warm[:], in_=warm[:], func=ACT.Sigmoid)
 
+        zero_values = grouped.tile([P, ZERO_WIDTH * PACK], BF16, tag="self_t", align_bytes=64)
+        zero_codes = const.tile([P, ZERO_WIDTH], U32, align_bytes=64)
+        zero_scales = const.tile([P, ZERO_WIDTH], U8, align_bytes=64)
+        nc.vector.memset(zero_values[:], 0.0)
+        nc.vector.quantize_mx(
+            out=zero_codes[:].bitcast(FP8X4), scales=zero_scales[:], in_=zero_values[:]
+        )
+
         w_grouped = const.tile([P, 2, COLS, PACK], BF16, align_bytes=64)
         nc.vector.tensor_copy(out=w_grouped[:], in_=w_raw[:].rearrange("p i t f -> p i f t"))
         w_codes = const.tile([P, 2 * COLS], U32, align_bytes=64)
@@ -94,14 +104,23 @@ def tile_dogtaitujuanji_pb_t_kernel(tc, h_sage, w1b, w2b, gamma, beta, out):
         def banks_of(n_tiles):
             return [(first, min(BANK_TILES, n_tiles - first)) for first in range(0, n_tiles, BANK_TILES)]
 
-        def turn_piece(i):
+        def add_hops(i):
             h_piece = h_pieces[i]
             n_tiles = PIECES[i]
             sum_rows = grouped.tile([P, n_tiles, FEATS], BF16, tag="sum_rows")
-            nc.vector.tensor_tensor(
-                out=sum_rows[:], in0=h_piece[:, :, 1, :], in1=h_piece[:, :, 2, :], op=ALU.add
-            )
+            for first, count in banks_of(n_tiles):
+                tiles = slice(first, first + count)
+                nc.vector.tensor_tensor(
+                    out=sum_rows[:, tiles, :],
+                    in0=h_piece[:, tiles, 1, :],
+                    in1=h_piece[:, tiles, 2, :],
+                    op=ALU.add,
+                )
+            return sum_rows
 
+        def turn_self(i):
+            h_piece = h_pieces[i]
+            n_tiles = PIECES[i]
             self_t = grouped.tile([P, n_tiles * P * PACK], BF16, tag="self_t", align_bytes=64)
             for first, count in banks_of(n_tiles):
                 bank = psum_turn.tile([P, HALVES * count * P], F32, tag="turn")
@@ -118,7 +137,10 @@ def tile_dogtaitujuanji_pb_t_kernel(tc, h_sage, w1b, w2b, gamma, beta, out):
                     .rearrange("p (c u) -> p c u", u=HALVES)[:, first * P : (first + count) * P, :],
                     in_=bank[:].rearrange("p (u c) -> p c u", u=HALVES),
                 )
+            return self_t
 
+        def turn_neigh(i, sum_rows):
+            n_tiles = PIECES[i]
             neigh_t = grouped.tile([P, n_tiles * P * PACK], BF16, tag="neigh_t", align_bytes=64)
             for first, count in banks_of(n_tiles):
                 bank = psum_turn.tile([P, count * PACK * P], BF16, tag="turn")
@@ -137,7 +159,7 @@ def tile_dogtaitujuanji_pb_t_kernel(tc, h_sage, w1b, w2b, gamma, beta, out):
                     in_=bank[:].rearrange("p (g t c) -> p g c t", g=count, t=PACK),
                     mul=0.5,
                 )
-            return self_t, neigh_t
+            return neigh_t
 
         def quantise_piece(i, values):
             width = PIECES[i] * P
@@ -151,8 +173,20 @@ def tile_dogtaitujuanji_pb_t_kernel(tc, h_sage, w1b, w2b, gamma, beta, out):
                 operands.append((words, scales))
             return operands
 
-        def multiply_piece(i, operands):
-            y_psum = psum_y.tile([P, PIECES[i] * P], F32, tag="y")
+        def keep_clock(y_psum):
+            width = y_psum.shape[1]
+            for n in range(KEEP_PASSES):
+                nc.tensor.matmul_mx(
+                    out=y_psum[:],
+                    lhsT=zero_codes[:, :COLS].bitcast(FP8X4),
+                    lhsT_scale=zero_scales[:, :COLS],
+                    rhs=zero_codes[:, :width].bitcast(FP8X4),
+                    rhs_scale=zero_scales[:, :width],
+                    start=True,
+                    stop=True,
+                )
+
+        def multiply_piece(operands, y_psum):
             for w_index, (words, scales) in enumerate(operands):
                 w_cols = slice(w_index * COLS, (w_index + 1) * COLS)
                 nc.tensor.matmul_mx(
@@ -164,7 +198,6 @@ def tile_dogtaitujuanji_pb_t_kernel(tc, h_sage, w1b, w2b, gamma, beta, out):
                     start=(w_index == 0),
                     stop=(w_index == 1),
                 )
-            return y_psum
 
         def measure_piece(i, y_psum):
             nc.vector.bn_stats(out=stats[:, i, :], in_=y_psum[:])
@@ -178,11 +211,20 @@ def tile_dogtaitujuanji_pb_t_kernel(tc, h_sage, w1b, w2b, gamma, beta, out):
         products = {}
         y_pieces = []
         for step in range(n_pieces + 2):
-            if step < n_pieces:
-                turned[step] = turn_piece(step)
-            if 1 <= step <= n_pieces:
-                operands = quantise_piece(step - 1, turned[step - 1])
-                products[step - 1] = multiply_piece(step - 1, operands)
+            turning = step < n_pieces
+            multiplying = 1 <= step <= n_pieces
+            if turning:
+                sum_rows = add_hops(step)
+                self_t = turn_self(step)
+            if multiplying:
+                y_psum = psum_y.tile([P, PIECES[step - 1] * P], F32, tag="y")
+                products[step - 1] = y_psum
+            if turning and multiplying:
+                keep_clock(y_psum)
+            if turning:
+                turned[step] = (self_t, turn_neigh(step, sum_rows))
+            if multiplying:
+                multiply_piece(quantise_piece(step - 1, turned[step - 1]), y_psum)
             if step >= 2:
                 y_pieces.append(measure_piece(step - 2, products[step - 2]))
 

@@ -25,8 +25,6 @@ BN_STATS_DIM = 6
 TILES = ITEMS // P
 BANK_TILES = 2
 PIECES = (1, 1, 2) + (4,) * 9
-KEEP_PASSES = 2
-ZERO_WIDTH = 512
 Y_KEPT = 4
 assert sum(PIECES) == TILES
 
@@ -80,14 +78,6 @@ def tile_dogtaitujuanji_pb_t_kernel(tc, h_sage, w1b, w2b, gamma, beta, out):
         warm = const.tile([P, 1], F32)
         nc.vector.memset(warm[:], 0.0)
         nc.scalar.activation(out=warm[:], in_=warm[:], func=ACT.Sigmoid)
-
-        zero_values = grouped.tile([P, ZERO_WIDTH * PACK], BF16, tag="self_t", align_bytes=64)
-        zero_codes = const.tile([P, ZERO_WIDTH], U32, align_bytes=64)
-        zero_scales = const.tile([P, ZERO_WIDTH], U8, align_bytes=64)
-        nc.vector.memset(zero_values[:], 0.0)
-        nc.vector.quantize_mx(
-            out=zero_codes[:].bitcast(FP8X4), scales=zero_scales[:], in_=zero_values[:]
-        )
 
         w_grouped = const.tile([P, 2, COLS, PACK], BF16, align_bytes=64)
         nc.vector.tensor_copy(out=w_grouped[:], in_=w_raw[:].rearrange("p i t f -> p i f t"))
@@ -173,19 +163,6 @@ def tile_dogtaitujuanji_pb_t_kernel(tc, h_sage, w1b, w2b, gamma, beta, out):
                 operands.append((words, scales))
             return operands
 
-        def keep_clock(y_psum):
-            width = y_psum.shape[1]
-            for n in range(KEEP_PASSES):
-                nc.tensor.matmul_mx(
-                    out=y_psum[:],
-                    lhsT=zero_codes[:, :COLS].bitcast(FP8X4),
-                    lhsT_scale=zero_scales[:, :COLS],
-                    rhs=zero_codes[:, :width].bitcast(FP8X4),
-                    rhs_scale=zero_scales[:, :width],
-                    start=True,
-                    stop=True,
-                )
-
         def multiply_piece(operands, y_psum):
             for w_index, (words, scales) in enumerate(operands):
                 w_cols = slice(w_index * COLS, (w_index + 1) * COLS)
@@ -215,15 +192,10 @@ def tile_dogtaitujuanji_pb_t_kernel(tc, h_sage, w1b, w2b, gamma, beta, out):
             multiplying = 1 <= step <= n_pieces
             if turning:
                 sum_rows = add_hops(step)
-                self_t = turn_self(step)
+                turned[step] = (turn_self(step), turn_neigh(step, sum_rows))
             if multiplying:
                 y_psum = psum_y.tile([P, PIECES[step - 1] * P], F32, tag="y")
                 products[step - 1] = y_psum
-            if turning and multiplying:
-                keep_clock(y_psum)
-            if turning:
-                turned[step] = (self_t, turn_neigh(step, sum_rows))
-            if multiplying:
                 multiply_piece(quantise_piece(step - 1, turned[step - 1]), y_psum)
             if step >= 2:
                 y_pieces.append(measure_piece(step - 2, products[step - 2]))

from contextlib import ExitStack

import concourse.mybir as mybir
from concourse.masks import make_identity

BF16 = mybir.dt.bfloat16
F32 = mybir.dt.float32
U32 = mybir.dt.uint32
U8 = mybir.dt.uint8
FP8X4 = mybir.dt.float8_e4m3fn_x4
ALU = mybir.AluOpType
ACT = mybir.ActivationFunctionType

P = 128
PACK = 4
HALVES = 2
PAIR = 2
ITEMS = 5120
HOPS = 3
FEATS = 512
COLS = 128
BN_EPS = 1e-5
BN_STATS_DIM = 6

TILES = ITEMS // P
BANK_TILES = 2
PIECES = (1, 1, 2) + (4,) * 9
Y_KEPT = 4
assert sum(PIECES) == TILES

FLOPS = 2 * 2 * ITEMS * FEATS * COLS


def tile_dogtaitujuanji_pb_t_kernel(tc, h_sage, w1b, w2b, gamma, beta, out):
    nc = tc.nc
    h_rows = h_sage.rearrange("(p j) q k -> p j q k", j=TILES)
    out_rows = out.rearrange("(p j) f -> p j f", j=TILES)
    n_pieces = len(PIECES)
    first_tile = [sum(PIECES[:i]) for i in range(n_pieces)]

    with ExitStack() as ctx:
        ctx.enter_context(tc.manual_schedule())
        const = ctx.enter_context(tc.tile_pool(name="const", bufs=1))
        h_pool = ctx.enter_context(tc.tile_pool(name="h", bufs=1))
        y_pool = ctx.enter_context(tc.tile_pool(name="y_sbuf", bufs=1))
        grouped = ctx.enter_context(tc.tile_pool(name="grouped", bufs=3))
        packed = ctx.enter_context(tc.tile_pool(name="packed", bufs=3))
        result = ctx.enter_context(tc.tile_pool(name="result", bufs=3))
        rows_pool = ctx.enter_context(tc.tile_pool(name="rows", bufs=1))
        psum_turn = ctx.enter_context(tc.psum_pool(name="psum_turn", bufs=4))
        psum_y = ctx.enter_context(tc.psum_pool(name="psum_y", bufs=Y_KEPT))

        h_pieces = []
        for i, n_tiles in enumerate(PIECES):
            h_piece = h_pool.tile([P, n_tiles, HOPS, FEATS], BF16, name="h_piece%d" % i)
            nc.sync.dma_start(
                out=h_piece[:], in_=h_rows[:, first_tile[i] : first_tile[i] + n_tiles]
            )
            h_pieces.append(h_piece)

        w_raw = const.tile([P, 2, PACK, COLS], BF16)
        nc.scalar.dma_start(
            out=w_raw[:, 0].rearrange("p (u e) f -> p u (e f)", u=HALVES),
            in_=w2b.rearrange("(u p e) f -> p u (e f)", u=HALVES, e=PAIR),
        )
        nc.scalar.dma_start(out=w_raw[:, 1], in_=w1b.rearrange("(t p) f -> p t f", p=P))
        gamma_bf = const.tile([P, 1], BF16)
        beta_bf = const.tile([P, 1], BF16)
        nc.scalar.dma_start(out=gamma_bf[:], in_=gamma.rearrange("(f o) -> f o", o=1))
        nc.scalar.dma_start(out=beta_bf[:], in_=beta.rearrange("(f o) -> f o", o=1))

        ident_f32 = const.tile([P, P], F32)
        make_identity(nc, ident_f32[:])
        ident_bf16 = const.tile([P, P], BF16)
        make_identity(nc, ident_bf16[:])
        minus_half = const.tile([P, 1], F32)
        nc.vector.memset(minus_half[:], -0.5)
        warm = const.tile([P, 1], F32)
        nc.vector.memset(warm[:], 0.0)
        nc.scalar.activation(out=warm[:], in_=warm[:], func=ACT.Sigmoid)

        w_grouped = const.tile([P, 2, COLS, PACK], BF16, align_bytes=64)
        nc.vector.tensor_copy(out=w_grouped[:], in_=w_raw[:].rearrange("p i t f -> p i f t"))
        w_codes = const.tile([P, 2 * COLS], U32, align_bytes=64)
        w_scales = const.tile([P, 2 * COLS], U8, align_bytes=64)
        nc.vector.quantize_mx(
            out=w_codes[:].bitcast(FP8X4),
            scales=w_scales[:],
            in_=w_grouped[:].rearrange("p i f t -> p (i f t)"),
        )

        stats = const.tile([P, n_pieces, BN_STATS_DIM], F32)

        def banks_of(n_tiles):
            return [(first, min(BANK_TILES, n_tiles - first)) for first in range(0, n_tiles, BANK_TILES)]

        def add_hops(i):
            h_piece = h_pieces[i]
            n_tiles = PIECES[i]
            sum_rows = grouped.tile([P, n_tiles, FEATS], BF16, tag="sum_rows")
            for first, count in banks_of(n_tiles):
                tiles = slice(first, first + count)
                nc.vector.tensor_tensor(
                    out=sum_rows[:, tiles, :],
                    in0=h_piece[:, tiles, 1, :],
                    in1=h_piece[:, tiles, 2, :],
                    op=ALU.add,
                )
            return sum_rows

        def turn_self(i):
            h_piece = h_pieces[i]
            n_tiles = PIECES[i]
            self_t = grouped.tile([P, n_tiles * P * PACK], BF16, tag="self_t", align_bytes=64)
            for first, count in banks_of(n_tiles):
                bank = psum_turn.tile([P, HALVES * count * P], F32, tag="turn")
                for g in range(count):
                    words = h_piece[:, first + g, 0, :].bitcast(F32)
                    for u in range(HALVES):
                        at = (u * count + g) * P
                        nc.tensor.transpose(
                            bank[:, at : at + P], words[:, u * P : (u + 1) * P], ident_f32[:]
                        )
                nc.scalar.copy(
                    out=self_t[:]
                    .bitcast(F32)
                    .rearrange("p (c u) -> p c u", u=HALVES)[:, first * P : (first + count) * P, :],
                    in_=bank[:].rearrange("p (u c) -> p c u", u=HALVES),
                )
            return self_t

        def turn_neigh(i, sum_rows):
            n_tiles = PIECES[i]
            neigh_t = grouped.tile([P, n_tiles * P * PACK], BF16, tag="neigh_t", align_bytes=64)
            for first, count in banks_of(n_tiles):
                bank = psum_turn.tile([P, count * PACK * P], BF16, tag="turn")
                for g in range(count):
                    for t in range(PACK):
                        at = (g * PACK + t) * P
                        nc.tensor.transpose(
                            bank[:, at : at + P],
                            sum_rows[:, first + g, t * P : (t + 1) * P],
                            ident_bf16[:],
                        )
                nc.scalar.mul(
                    out=neigh_t[:].rearrange("p (g c t) -> p g c t", c=P, t=PACK)[
                        :, first : first + count
                    ],
                    in_=bank[:].rearrange("p (g t c) -> p g c t", g=count, t=PACK),
                    mul=0.5,
                )
            return neigh_t

        def quantise_piece(i, values):
            width = PIECES[i] * P
            operands = []
            for name, tile_bf16 in zip(("self", "neigh"), values):
                words = packed.tile([P, width], U32, tag=name + "_codes", align_bytes=64)
                scales = packed.tile([P, width], U8, tag=name + "_scales", align_bytes=64)
                nc.vector.quantize_mx(
                    out=words[:].bitcast(FP8X4), scales=scales[:], in_=tile_bf16[:]
                )
                operands.append((words, scales))
            return operands

        def multiply_piece(operands, y_psum):
            for w_index, (words, scales) in enumerate(operands):
                w_cols = slice(w_index * COLS, (w_index + 1) * COLS)
                nc.tensor.matmul_mx(
                    out=y_psum[:],
                    lhsT=w_codes[:, w_cols].bitcast(FP8X4),
                    lhsT_scale=w_scales[:, w_cols],
                    rhs=words[:].bitcast(FP8X4),
                    rhs_scale=scales[:],
                    start=(w_index == 0),
                    stop=(w_index == 1),
                )

        def measure_piece(i, y_psum):
            nc.vector.bn_stats(out=stats[:, i, :], in_=y_psum[:])
            if i >= n_pieces - Y_KEPT:
                return y_psum
            y_sbuf = y_pool.tile([P, PIECES[i] * P], F32, name="y_sbuf%d" % i)
            nc.vector.tensor_copy(out=y_sbuf[:], in_=y_psum[:])
            return y_sbuf

        turned = {}
        products = {}
        y_pieces = []
        for step in range(n_pieces + 2):
            turning = step < n_pieces
            multiplying = 1 <= step <= n_pieces
            if turning:
                sum_rows = add_hops(step)
                turned[step] = (turn_self(step), turn_neigh(step, sum_rows))
            if multiplying:
                y_psum = psum_y.tile([P, PIECES[step - 1] * P], F32, tag="y")
                products[step - 1] = y_psum
                multiply_piece(quantise_piece(step - 1, turned[step - 1]), y_psum)
            if step >= 2:
                y_pieces.append(measure_piece(step - 2, products[step - 2]))

        gamma_f = const.tile([P, 1], F32)
        neg_gamma_f = const.tile([P, 1], F32)
        beta_f = const.tile([P, 1], F32)
        mean_var = const.tile([P, 2], F32)
        var_eps = const.tile([P, 1], F32)
        neg_gamma_mean = const.tile([P, 1], F32)
        rstd = const.tile([P, 1], F32)
        gain = const.tile([P, 1], F32)
        shift = const.tile([P, 1], F32)
        nc.vector.bn_aggr(out=mean_var[:], in_=stats[:].rearrange("p i s -> p (i s)"))
        nc.vector.tensor_scalar_add(out=var_eps[:], in0=mean_var[:, 1:2], scalar1=BN_EPS)
        nc.gpsimd.tensor_tensor(out=rstd[:], in0=var_eps[:], in1=minus_half[:], op=ALU.pow)
        nc.vector.tensor_copy(out=gamma_f[:], in_=gamma_bf[:])
        nc.vector.tensor_copy(out=beta_f[:], in_=beta_bf[:])
        nc.vector.tensor_scalar_mul(out=neg_gamma_f[:], in0=gamma_bf[:], scalar1=-1.0)
        nc.vector.tensor_mul(out=neg_gamma_mean[:], in0=mean_var[:, 0:1], in1=neg_gamma_f[:])
        nc.vector.tensor_mul(out=gain[:], in0=gamma_f[:], in1=rstd[:])
        nc.vector.tensor_scalar(
            out=shift[:],
            in0=neg_gamma_mean[:],
            scalar1=rstd[:, 0:1],
            scalar2=beta_f[:, 0:1],
            op0=ALU.mult,
            op1=ALU.add,
        )

        for i, n_tiles in enumerate(PIECES):
            sig = result.tile([P, n_tiles * P], F32, tag="sig")
            nc.scalar.activation(
                out=sig[:],
                in_=y_pieces[i][:],
                func=ACT.Sigmoid,
                bias=shift[:, 0:1],
                scale=gain[:, 0:1],
            )
            back = psum_turn.tile([P, n_tiles, COLS], F32, tag="turn")
            for g in range(n_tiles):
                nc.tensor.transpose(back[:, g, :], sig[:, g * P : (g + 1) * P], ident_f32[:])
            rows = rows_pool.tile([P, n_tiles, COLS], F32, name="rows%d" % i)
            nc.vector.tensor_copy(out=rows[:], in_=back[:])
            nc.sync.dma_start(
                out=out_rows[:, first_tile[i] : first_tile[i] + n_tiles, :], in_=rows[:]
            )
